import numpy as np
import ml_dtypes


def mxq(x, axis, fmt="e4m3"):
    dtype, down = {"e4m3": (ml_dtypes.float8_e4m3fn, 7), "e5m2": (ml_dtypes.float8_e5m2, 14)}[fmt]
    v = np.moveaxis(np.asarray(x, np.float32).astype(ml_dtypes.bfloat16).astype(np.float64), axis, -1)
    blocks = v.reshape(v.shape[:-1] + (-1, 32))
    amax = np.abs(blocks).max(-1, keepdims=True)
    byte = np.maximum(np.where(amax > 0, np.frexp(amax)[1] - 1 + 127, 0) - down, 1)
    scale = np.exp2(byte - 127.0)
    codes = (blocks / scale).astype(np.float32).astype(dtype).astype(np.float64)
    return np.moveaxis((codes * scale).reshape(v.shape), -1, axis)


WIDE = False


def mx_kscale(k):
    if not WIDE:
        return np.ones(k)
    levels = np.array([30, -30])
    if k % 512:
        return np.exp2(np.random.permutation(np.resize(levels, k // 32))).repeat(32)
    a = np.empty((k // 512, 16))
    for p in range(k // 512):
        a[p, :8] = np.random.permutation(np.resize(levels, 8))
        for g in range(8):
            far = levels[np.abs(levels - a[p, g]) >= 10]
            a[p, g + 8] = far[np.random.randint(len(far))]
    return np.exp2(a.ravel()).repeat(32)


BF16 = ml_dtypes.bfloat16


def bf(x):
    return np.asarray(x, np.float32).astype(BF16)


def f64(x):
    return np.asarray(x).astype(np.float64)


B, N, G, L = 1024, 512, 128, 768
N2 = 2 * N


def setup_inputs():
    s = mx_kscale(N2)
    return {
        "Volt": bf(np.random.standard_normal((B, N2)) * s),
        "Y": bf(np.random.standard_normal((N2, N2)) / np.sqrt(N2) / s[None, :] / s[:, None]),
        "Yconj": bf(np.random.standard_normal((N2, N2)) / np.sqrt(N2) / s[None, :] / s[:, None]),
    }


def reference(Volt, Y, Yconj):
    v = f64(Volt)
    vq = mxq(v, 1, "e5m2")
    quad_p = v * (vq @ mxq(f64(Y), 1, "e4m3").T)
    quad_q = v * (vq @ mxq(f64(Yconj), 1, "e4m3").T)
    return quad_p, quad_q

@@ -1,0 +1,173 @@
+from contextlib import ExitStack
+
+import concourse.mybir as mybir
+from concourse.masks import make_identity
+
+B = 1024
+K = 1024
+R = 1024
+FLOPS = 2 * 2 * B * K * R
+
+F32 = mybir.dt.float32
+BF16 = mybir.dt.bfloat16
+U32 = mybir.dt.uint32
+U8 = mybir.dt.uint8
+E4M3 = mybir.dt.float8_e4m3fn_x4
+E5M2 = mybir.dt.float8_e5m2_x4
+
+P = 128
+SLOTS = 2
+ROWS = P * SLOTS
+PASSES = K // 512
+WORDS = 256
+N_TILE = 512
+
+
+def tile_pinnlayer_pb_kernel(tc, Volt, Y, Yconj, out_0, out_1):
+    nc = tc.nc
+    weights = (Y, Yconj)
+    outs = (out_0, out_1)
+
+    with ExitStack() as ctx:
+        keep = ctx.enter_context(tc.tile_pool(name="keep", bufs=1))
+        stage = ctx.enter_context(tc.tile_pool(name="stage", bufs=6))
+        psum = ctx.enter_context(tc.psum_pool(name="psum", bufs=4))
+        ctx.enter_context(tc.manual_schedule())
+
+        raw = {}
+
+        def load(unit):
+            kind, idx = unit
+            src = Volt if kind == "v" else weights[kind]
+            t = keep.tile([P, SLOTS, K], BF16, name="raw_%s_%d" % (kind, idx), align_bytes=64)
+            nc.sync.dma_start(
+                out=t[:], in_=src[idx * ROWS : (idx + 1) * ROWS, :].rearrange("(p j) k -> p j k", j=SLOTS)
+            )
+            raw[unit] = t
+
+        order = [("v", 0), (0, 0), (0, 1), ("v", 1), (0, 2), (0, 3), ("v", 2), ("v", 3), (1, 0), (1, 1), (1, 2), (1, 3)]
+        for unit in order:
+            load(unit)
+
+        ident = keep.tile([P, P], F32, name="ident")
+        make_identity(nc, ident[:])
+
+        codes = {}
+        scales = {}
+        for a in range(4):
+            for g in range(PASSES):
+                codes["v", a, g] = keep.tile([P, ROWS], U32, name="vc_%d_%d" % (a, g), align_bytes=64)
+                scales["v", a, g] = keep.tile([P, ROWS], U8, name="vs_%d_%d" % (a, g), align_bytes=64)
+        for o in range(2):
+            for h in range(2):
+                for g in range(PASSES):
+                    codes[o, h, g] = keep.tile([P, N_TILE], U32, name="wc_%d_%d_%d" % (o, h, g), align_bytes=64)
+                    scales[o, h, g] = keep.tile([P, N_TILE], U8, name="ws_%d_%d_%d" % (o, h, g), align_bytes=64)
+        res = {}
+        for o in range(2):
+            for a in range(4):
+                res[o, a] = keep.tile([P, SLOTS, R], F32, name="res_%d_%d" % (o, a))
+
+        def prepare(unit):
+            kind, idx = unit
+            grouped = []
+            for g in range(PASSES):
+                bank = psum.tile([P, SLOTS, 2, P], F32, tag="turned")
+                for j in range(SLOTS):
+                    words = raw[unit][:, j, :].bitcast(F32)
+                    for u in range(2):
+                        nc.tensor.transpose(
+                            bank[:, j, u, :], words[:, WORDS * g + u : WORDS * (g + 1) : 2], ident[:]
+                        )
+                grp = stage.tile([P, 4 * ROWS], BF16, tag="grouped", align_bytes=64)
+                if kind == "v":
+                    nc.scalar.copy(
+                        out=grp[:].bitcast(F32).rearrange("p (j q u) -> p j q u", j=SLOTS, u=2),
+                        in_=bank[:].rearrange("p j u q -> p j q u"),
+                    )
+                else:
+                    nc.scalar.copy(
+                        out=grp[:].bitcast(F32).rearrange("p (q j u) -> p q j u", j=SLOTS, u=2),
+                        in_=bank[:].rearrange("p j u q -> p q j u"),
+                    )
+                grouped.append(grp)
+            for g in range(PASSES):
+                if kind == "v":
+                    nc.vector.quantize_mx(
+                        out=codes["v", idx, g][:].bitcast(E5M2), scales=scales["v", idx, g][:], in_=grouped[g][:]
+                    )
+                else:
+                    cols = slice((idx % 2) * ROWS, (idx % 2 + 1) * ROWS)
+                    nc.vector.quantize_mx(
+                        out=codes[kind, idx // 2, g][:, cols].bitcast(E4M3),
+                        scales=scales[kind, idx // 2, g][:, cols],
+                        in_=grouped[g][:],
+                    )
+
+        def product(o, a, j, h):
+            acc = psum.tile([P, N_TILE], F32, tag="acc")
+            m = slice(j * P, (j + 1) * P)
+            for g in range(PASSES):
+                nc.tensor.matmul_mx(
+                    out=acc[:],
+                    lhsT=codes["v", a, g][:, m].bitcast(E5M2),
+                    lhsT_scale=scales["v", a, g][:, m],
+                    rhs=codes[o, h, g][:].bitcast(E4M3),
+                    rhs_scale=scales[o, h, g][:],
+                    start=(g == 0),
+                    stop=(g == PASSES - 1),
+                )
+            n = slice(h * N_TILE, (h + 1) * N_TILE)
+            nc.vector.tensor_tensor(
+                out=res[o, a][:, j, n], in0=acc[:], in1=raw["v", a][:, j, n], op=mybir.AluOpType.mult
+            )
+
+        def store(o, a, js, n):
+            dst = outs[o][a * ROWS : (a + 1) * ROWS, :].rearrange("(p j) r -> p j r", j=SLOTS)
+            nc.sync.dma_start(out=dst[:, js, n], in_=res[o, a][:, js, n])
+
+        whole = slice(0, R)
+        both = slice(0, SLOTS)
+
+        def half(o, a, h):
+            for j in range(SLOTS):
+                product(o, a, j, h)
+
+        def row(o, a, j):
+            for h in range(2):
+                product(o, a, j, h)
+            store(o, a, slice(j, j + 1), whole)
+
+        prepare(("v", 0))
+        prepare((0, 0))
+        prepare((0, 1))
+        prepare(("v", 1))
+        half(0, 0, 0)
+        prepare((0, 2))
+        half(0, 1, 0)
+        prepare((0, 3))
+        prepare(("v", 2))
+        half(0, 0, 1)
+        store(0, 0, both, whole)
+        half(0, 1, 1)
+        store(0, 1, both, whole)
+        prepare(("v", 3))
+        row(0, 2, 0)
+        row(0, 2, 1)
+        prepare((1, 0))
+        row(0, 3, 0)
+        prepare((1, 1))
+        row(0, 3, 1)
+        prepare((1, 2))
+        for a in range(4):
+            if a == 2:
+                prepare((1, 3))
+            half(1, a, 0)
+            store(1, a, both, slice(0, N_TILE))
+        for a in range(4):
+            for j in range(SLOTS):
+                product(1, a, j, 1)
+                if a == 3:
+                    store(1, a, slice(j, j + 1), slice(N_TILE, R))
+            if a < 3:
+                store(1, a, both, slice(N_TILE, R))

@@ -68,17 +68,28 @@ def tile_pinnlayer_pb_kernel(tc, Volt, Y, Yconj, out_0, out_1):
             for a in range(4):
                 res[o, a] = keep.tile([P, SLOTS, R], F32, name="res_%d_%d" % (o, a))
 
-        def prepare(unit):
+        split = {}
+        grouped = {}
+
+        def deinterleave(unit):
+            t = stage.tile([P, 2, SLOTS * PASSES * P], F32, tag="split", bufs=4)
+            words = raw[unit][:].rearrange("p j k -> p (j k)").bitcast(F32)
+            nc.scalar.copy(out=t[:], in_=words.rearrange("p (n u) -> p u n", u=2))
+            split[unit] = t
+
+        def turn(unit):
             kind, idx = unit
-            grouped = []
             for g in range(PASSES):
                 bank = psum.tile([P, SLOTS, 2, P], F32, tag="turned")
                 for j in range(SLOTS):
-                    words = raw[unit][:, j, :].bitcast(F32)
                     for u in range(2):
-                        nc.tensor.transpose(
-                            bank[:, j, u, :], words[:, WORDS * g + u : WORDS * (g + 1) : 2], ident[:]
-                        )
+                        if unit in split:
+                            first = (j * PASSES + g) * P
+                            src = split[unit][:, u, first : first + P]
+                        else:
+                            words = raw[unit][:, j, :].bitcast(F32)
+                            src = words[:, WORDS * g + u : WORDS * (g + 1) : 2]
+                        nc.tensor.transpose(bank[:, j, u, :], src, ident[:])
                 grp = stage.tile([P, 4 * ROWS], BF16, tag="grouped", align_bytes=64)
                 if kind == "v":
                     nc.scalar.copy(
@@ -90,19 +101,21 @@ def tile_pinnlayer_pb_kernel(tc, Volt, Y, Yconj, out_0, out_1):
                         out=grp[:].bitcast(F32).rearrange("p (q j u) -> p q j u", j=SLOTS, u=2),
                         in_=bank[:].rearrange("p j u q -> p q j u"),
                     )
-                grouped.append(grp)
-            for g in range(PASSES):
-                if kind == "v":
-                    nc.vector.quantize_mx(
-                        out=codes["v", idx, g][:].bitcast(E5M2), scales=scales["v", idx, g][:], in_=grouped[g][:]
-                    )
-                else:
-                    cols = slice((idx % 2) * ROWS, (idx % 2 + 1) * ROWS)
-                    nc.vector.quantize_mx(
-                        out=codes[kind, idx // 2, g][:, cols].bitcast(E4M3),
-                        scales=scales[kind, idx // 2, g][:, cols],
-                        in_=grouped[g][:],
-                    )
+                grouped[unit, g] = grp
+
+        def quantise(unit, g):
+            kind, idx = unit
+            if kind == "v":
+                nc.vector.quantize_mx(
+                    out=codes["v", idx, g][:].bitcast(E5M2), scales=scales["v", idx, g][:], in_=grouped[unit, g][:]
+                )
+            else:
+                cols = slice((idx % 2) * ROWS, (idx % 2 + 1) * ROWS)
+                nc.vector.quantize_mx(
+                    out=codes[kind, idx // 2, g][:, cols].bitcast(E4M3),
+                    scales=scales[kind, idx // 2, g][:, cols],
+                    in_=grouped[unit, g][:],
+                )
 
         def product(o, a, j, h):
             acc = psum.tile([P, N_TILE], F32, tag="acc")
@@ -126,48 +139,37 @@ def tile_pinnlayer_pb_kernel(tc, Volt, Y, Yconj, out_0, out_1):
             dst = outs[o][a * ROWS : (a + 1) * ROWS, :].rearrange("(p j) r -> p j r", j=SLOTS)
             nc.sync.dma_start(out=dst[:, js, n], in_=res[o, a][:, js, n])
 
-        whole = slice(0, R)
-        both = slice(0, SLOTS)
+        def tile_and_store(o, a, j, h, by_half):
+            product(o, a, j, h)
+            if by_half:
+                store(o, a, slice(j, j + 1), slice(h * N_TILE, (h + 1) * N_TILE))
+            elif h == 1:
+                store(o, a, slice(j, j + 1), slice(0, R))
 
-        def half(o, a, h):
-            for j in range(SLOTS):
-                product(o, a, j, h)
-
-        def row(o, a, j):
+        groups = []
+        for o in range(2):
             for h in range(2):
-                product(o, a, j, h)
-            store(o, a, slice(j, j + 1), whole)
+                groups.append([(o, a, j, h, o == 1) for a in range(2) for j in range(SLOTS)])
+            for a in range(2, 4):
+                groups.append([(o, a, j, h, (o, a, j) == (1, 3, 1)) for j in range(SLOTS) for h in range(2)])
 
-        prepare(("v", 0))
-        prepare((0, 0))
-        prepare((0, 1))
-        prepare(("v", 1))
-        half(0, 0, 0)
-        prepare((0, 2))
-        half(0, 1, 0)
-        prepare((0, 3))
-        prepare(("v", 2))
-        half(0, 0, 1)
-        store(0, 0, both, whole)
-        half(0, 1, 1)
-        store(0, 1, both, whole)
-        prepare(("v", 3))
-        row(0, 2, 0)
-        row(0, 2, 1)
-        prepare((1, 0))
-        row(0, 3, 0)
-        prepare((1, 1))
-        row(0, 3, 1)
-        prepare((1, 2))
-        for a in range(4):
-            if a == 2:
-                prepare((1, 3))
-            half(1, a, 0)
-            store(1, a, both, slice(0, N_TILE))
-        for a in range(4):
-            for j in range(SLOTS):
-                product(1, a, j, 1)
-                if a == 3:
-                    store(1, a, slice(j, j + 1), slice(N_TILE, R))
-            if a < 3:
-                store(1, a, both, slice(N_TILE, R))
+        turn_before = {0: order[4:6], 1: order[6:8], 3: order[8:10], 4: order[10:12]}
+        split_during = {0: order[6:8], 1: order[8:11], 3: order[11:12]}
+        quantise_before_tile = (2, 1, 1, 0)
+
+        for unit in order[:4]:
+            turn(unit)
+            for g in range(PASSES):
+                quantise(unit, g)
+        for n, group in enumerate(groups):
+            pending = []
+            for unit in turn_before.get(n, []):
+                turn(unit)
+                pending.extend([(unit, g) for g in range(PASSES)])
+            for unit in split_during.get(n, []):
+                deinterleave(unit)
+            for i, tile in enumerate(group):
+                first = sum(quantise_before_tile[:i])
+                for unit, g in pending[first : first + quantise_before_tile[i]]:
+                    quantise(unit, g)
+                tile_and_store(*tile)

@@ -21,6 +21,7 @@ ROWS = P * SLOTS
 PASSES = K // 512
 WORDS = 256
 N_TILE = 512
+WARM_N = 256
 
 
 def tile_pinnlayer_pb_kernel(tc, Volt, Y, Yconj, out_0, out_1):
@@ -157,14 +158,26 @@ def tile_pinnlayer_pb_kernel(tc, Volt, Y, Yconj, out_0, out_1):
         split_during = {0: order[6:8], 1: order[8:11], 3: order[11:12]}
         quantise_before_tile = (2, 1, 1, 0)
 
+        idle = keep.tile([P, WARM_N], F32, name="idle")
+        nc.vector.memset(idle[:], 0.0)
+
+        def warm_up():
+            unread = psum.tile([P, N_TILE], F32, tag="acc")
+            nc.tensor.matmul(unread[:, :WARM_N], idle[:, :P], idle[:], start=True, stop=True)
+
+        for n in range(3):
+            warm_up()
         for unit in order[:4]:
             turn(unit)
+            warm_up()
             for g in range(PASSES):
                 quantise(unit, g)
         for n, group in enumerate(groups):
             pending = []
             for unit in turn_before.get(n, []):
                 turn(unit)
+                if unit == order[4]:
+                    warm_up()
                 pending.extend([(unit, g) for g in range(PASSES)])
             for unit in split_during.get(n, []):
                 deinterleave(unit)

@@ -22,6 +22,7 @@ PASSES = K // 512
 WORDS = 256
 N_TILE = 512
 WARM_N = 256
+HOLD_N = 384
 
 
 def tile_pinnlayer_pb_kernel(tc, Volt, Y, Yconj, out_0, out_1):
@@ -72,10 +73,10 @@ def tile_pinnlayer_pb_kernel(tc, Volt, Y, Yconj, out_0, out_1):
         split = {}
         grouped = {}
 
-        def deinterleave(unit):
+        def deinterleave(unit, copy):
             t = stage.tile([P, 2, SLOTS * PASSES * P], F32, tag="split", bufs=4)
             words = raw[unit][:].rearrange("p j k -> p (j k)").bitcast(F32)
-            nc.scalar.copy(out=t[:], in_=words.rearrange("p (n u) -> p u n", u=2))
+            copy(out=t[:], in_=words.rearrange("p (n u) -> p u n", u=2))
             split[unit] = t
 
         def turn(unit):
@@ -150,38 +151,49 @@ def tile_pinnlayer_pb_kernel(tc, Volt, Y, Yconj, out_0, out_1):
         groups = []
         for o in range(2):
             for h in range(2):
-                groups.append([(o, a, j, h, o == 1) for a in range(2) for j in range(SLOTS)])
+                groups.append([(o, a, j, h, True) for a in range(2) for j in range(SLOTS)])
             for a in range(2, 4):
-                groups.append([(o, a, j, h, (o, a, j) == (1, 3, 1)) for j in range(SLOTS) for h in range(2)])
-
-        turn_before = {0: order[4:6], 1: order[6:8], 3: order[8:10], 4: order[10:12]}
-        split_during = {0: order[6:8], 1: order[8:11], 3: order[11:12]}
-        quantise_before_tile = (2, 1, 1, 0)
+                groups.append([(o, a, j, h, o == 1) for j in range(SLOTS) for h in range(2)])
 
         idle = keep.tile([P, WARM_N], F32, name="idle")
         nc.vector.memset(idle[:], 0.0)
-
-        def warm_up():
-            unread = psum.tile([P, N_TILE], F32, tag="acc")
-            nc.tensor.matmul(unread[:, :WARM_N], idle[:, :P], idle[:], start=True, stop=True)
+        idle_bf16 = idle[:].bitcast(BF16)
 
         for n in range(3):
-            warm_up()
+            unread = psum.tile([P, N_TILE], F32, tag="acc")
+            nc.tensor.matmul(unread[:, :WARM_N], idle[:, :P], idle[:], start=True, stop=True)
         for unit in order[:4]:
             turn(unit)
-            warm_up()
+            unread = psum.tile([P, N_TILE], F32, tag="acc")
+            nc.tensor.matmul(unread[:, :HOLD_N], idle_bf16[:, :P], idle_bf16[:, :HOLD_N], start=True, stop=True)
             for g in range(PASSES):
                 quantise(unit, g)
-        for n, group in enumerate(groups):
+
+        deinterleave(order[5], nc.vector.tensor_copy)
+        turn(order[4])
+        deinterleave(order[6], nc.scalar.copy)
+        for g in range(PASSES):
+            quantise(order[4], g)
+        for tile in groups[0][:2]:
+            tile_and_store(*tile)
+        deinterleave(order[7], nc.vector.tensor_copy)
+        turn(order[5])
+        for g in range(PASSES):
+            quantise(order[5], g)
+        for tile in groups[0][2:]:
+            tile_and_store(*tile)
+
+        turn_before = {1: order[6:8], 3: order[8:10], 4: order[10:12]}
+        split_during = {1: order[8:11], 3: order[11:12]}
+        quantise_before_tile = (2, 1, 1, 0)
+        for n in range(1, len(groups)):
             pending = []
             for unit in turn_before.get(n, []):
                 turn(unit)
-                if unit == order[4]:
-                    warm_up()
                 pending.extend([(unit, g) for g in range(PASSES)])
             for unit in split_during.get(n, []):
-                deinterleave(unit)
-            for i, tile in enumerate(group):
+                deinterleave(unit, nc.scalar.copy)
+            for i, tile in enumerate(groups[n]):
                 first = sum(quantise_before_tile[:i])
                 for unit, g in pending[first : first + quantise_before_tile[i]]:
                     quantise(unit, g)

@@ -149,11 +149,13 @@ def tile_pinnlayer_pb_kernel(tc, Volt, Y, Yconj, out_0, out_1):
                 store(o, a, slice(j, j + 1), slice(0, R))
 
         groups = []
-        for o in range(2):
-            for h in range(2):
-                groups.append([(o, a, j, h, True) for a in range(2) for j in range(SLOTS)])
-            for a in range(2, 4):
-                groups.append([(o, a, j, h, o == 1) for j in range(SLOTS) for h in range(2)])
+        for h in range(2):
+            groups.append([(0, a, j, h, True) for a in range(2) for j in range(SLOTS)])
+        for a in range(2, 4):
+            groups.append([(0, a, j, h, False) for j in range(SLOTS) for h in range(2)])
+        for h in range(2):
+            for first in (0, 2):
+                groups.append([(1, a, j, h, True) for a in range(first, first + 2) for j in range(SLOTS)])
 
         idle = keep.tile([P, WARM_N], F32, name="idle")
         nc.vector.memset(idle[:], 0.0)
@@ -169,7 +171,6 @@ def tile_pinnlayer_pb_kernel(tc, Volt, Y, Yconj, out_0, out_1):
             for g in range(PASSES):
                 quantise(unit, g)
 
-        deinterleave(order[5], nc.vector.tensor_copy)
         turn(order[4])
         deinterleave(order[6], nc.scalar.copy)
         for g in range(PASSES):
@@ -183,9 +184,8 @@ def tile_pinnlayer_pb_kernel(tc, Volt, Y, Yconj, out_0, out_1):
         for tile in groups[0][2:]:
             tile_and_store(*tile)
 
-        turn_before = {1: order[6:8], 3: order[8:10], 4: order[10:12]}
+        turn_before = {1: order[6:8], 3: order[8:10], 4: order[10:11], 5: order[11:12]}
         split_during = {1: order[8:11], 3: order[11:12]}
-        quantise_before_tile = (2, 1, 1, 0)
         for n in range(1, len(groups)):
             pending = []
             for unit in turn_before.get(n, []):
@@ -193,6 +193,7 @@ def tile_pinnlayer_pb_kernel(tc, Volt, Y, Yconj, out_0, out_1):
                 pending.extend([(unit, g) for g in range(PASSES)])
             for unit in split_during.get(n, []):
                 deinterleave(unit, nc.scalar.copy)
+            quantise_before_tile = (2, 1, 1, 0) if len(pending) == 4 else (0, 1, 1, 0)
             for i, tile in enumerate(groups[n]):
                 first = sum(quantise_before_tile[:i])
                 for unit, g in pending[first : first + quantise_before_tile[i]]:

from contextlib import ExitStack

import concourse.mybir as mybir
from concourse.masks import make_identity

B = 1024
K = 1024
R = 1024
FLOPS = 2 * 2 * B * K * R

F32 = mybir.dt.float32
BF16 = mybir.dt.bfloat16
U32 = mybir.dt.uint32
U8 = mybir.dt.uint8
E4M3 = mybir.dt.float8_e4m3fn_x4
E5M2 = mybir.dt.float8_e5m2_x4

P = 128
SLOTS = 2
ROWS = P * SLOTS
PASSES = K // 512
WORDS = 256
N_TILE = 512
WARM_N = 256
HOLD_N = 384


def tile_pinnlayer_pb_kernel(tc, Volt, Y, Yconj, out_0, out_1):
    nc = tc.nc
    weights = (Y, Yconj)
    outs = (out_0, out_1)

    with ExitStack() as ctx:
        keep = ctx.enter_context(tc.tile_pool(name="keep", bufs=1))
        stage = ctx.enter_context(tc.tile_pool(name="stage", bufs=6))
        psum = ctx.enter_context(tc.psum_pool(name="psum", bufs=4))
        ctx.enter_context(tc.manual_schedule())

        raw = {}

        def load(unit):
            kind, idx = unit
            src = Volt if kind == "v" else weights[kind]
            t = keep.tile([P, SLOTS, K], BF16, name="raw_%s_%d" % (kind, idx), align_bytes=64)
            nc.sync.dma_start(
                out=t[:], in_=src[idx * ROWS : (idx + 1) * ROWS, :].rearrange("(p j) k -> p j k", j=SLOTS)
            )
            raw[unit] = t

        order = [("v", 0), (0, 0), (0, 1), ("v", 1), (0, 2), (0, 3), ("v", 2), ("v", 3), (1, 0), (1, 1), (1, 2), (1, 3)]
        for unit in order:
            load(unit)

        ident = keep.tile([P, P], F32, name="ident")
        make_identity(nc, ident[:])

        codes = {}
        scales = {}
        for a in range(4):
            for g in range(PASSES):
                codes["v", a, g] = keep.tile([P, ROWS], U32, name="vc_%d_%d" % (a, g), align_bytes=64)
                scales["v", a, g] = keep.tile([P, ROWS], U8, name="vs_%d_%d" % (a, g), align_bytes=64)
        for o in range(2):
            for h in range(2):
                for g in range(PASSES):
                    codes[o, h, g] = keep.tile([P, N_TILE], U32, name="wc_%d_%d_%d" % (o, h, g), align_bytes=64)
                    scales[o, h, g] = keep.tile([P, N_TILE], U8, name="ws_%d_%d_%d" % (o, h, g), align_bytes=64)
        res = {}
        for o in range(2):
            for a in range(4):
                res[o, a] = keep.tile([P, SLOTS, R], F32, name="res_%d_%d" % (o, a))

        split = {}
        grouped = {}

        def deinterleave(unit, copy):
            t = stage.tile([P, 2, SLOTS * PASSES * P], F32, tag="split", bufs=4)
            words = raw[unit][:].rearrange("p j k -> p (j k)").bitcast(F32)
            copy(out=t[:], in_=words.rearrange("p (n u) -> p u n", u=2))
            split[unit] = t

        def turn(unit):
            kind, idx = unit
            for g in range(PASSES):
                bank = psum.tile([P, SLOTS, 2, P], F32, tag="turned")
                for j in range(SLOTS):
                    for u in range(2):
                        if unit in split:
                            first = (j * PASSES + g) * P
                            src = split[unit][:, u, first : first + P]
                        else:
                            words = raw[unit][:, j, :].bitcast(F32)
                            src = words[:, WORDS * g + u : WORDS * (g + 1) : 2]
                        nc.tensor.transpose(bank[:, j, u, :], src, ident[:])
                grp = stage.tile([P, 4 * ROWS], BF16, tag="grouped", align_bytes=64)
                if kind == "v":
                    nc.scalar.copy(
                        out=grp[:].bitcast(F32).rearrange("p (j q u) -> p j q u", j=SLOTS, u=2),
                        in_=bank[:].rearrange("p j u q -> p j q u"),
                    )
                else:
                    nc.scalar.copy(
                        out=grp[:].bitcast(F32).rearrange("p (q j u) -> p q j u", j=SLOTS, u=2),
                        in_=bank[:].rearrange("p j u q -> p q j u"),
                    )
                grouped[unit, g] = grp

        def quantise(unit, g):
            kind, idx = unit
            if kind == "v":
                nc.vector.quantize_mx(
                    out=codes["v", idx, g][:].bitcast(E5M2), scales=scales["v", idx, g][:], in_=grouped[unit, g][:]
                )
            else:
                cols = slice((idx % 2) * ROWS, (idx % 2 + 1) * ROWS)
                nc.vector.quantize_mx(
                    out=codes[kind, idx // 2, g][:, cols].bitcast(E4M3),
                    scales=scales[kind, idx // 2, g][:, cols],
                    in_=grouped[unit, g][:],
                )

        def product(o, a, j, h):
            acc = psum.tile([P, N_TILE], F32, tag="acc")
            m = slice(j * P, (j + 1) * P)
            for g in range(PASSES):
                nc.tensor.matmul_mx(
                    out=acc[:],
                    lhsT=codes["v", a, g][:, m].bitcast(E5M2),
                    lhsT_scale=scales["v", a, g][:, m],
                    rhs=codes[o, h, g][:].bitcast(E4M3),
                    rhs_scale=scales[o, h, g][:],
                    start=(g == 0),
                    stop=(g == PASSES - 1),
                )
            n = slice(h * N_TILE, (h + 1) * N_TILE)
            nc.vector.tensor_tensor(
                out=res[o, a][:, j, n], in0=acc[:], in1=raw["v", a][:, j, n], op=mybir.AluOpType.mult
            )

        def store(o, a, js, n):
            dst = outs[o][a * ROWS : (a + 1) * ROWS, :].rearrange("(p j) r -> p j r", j=SLOTS)
            nc.sync.dma_start(out=dst[:, js, n], in_=res[o, a][:, js, n])

        def tile_and_store(o, a, j, h, by_half):
            product(o, a, j, h)
            if by_half:
                store(o, a, slice(j, j + 1), slice(h * N_TILE, (h + 1) * N_TILE))
            elif h == 1:
                store(o, a, slice(j, j + 1), slice(0, R))

        groups = []
        for h in range(2):
            groups.append([(0, a, j, h, True) for a in range(2) for j in range(SLOTS)])
        for a in range(2, 4):
            groups.append([(0, a, j, h, False) for j in range(SLOTS) for h in range(2)])
        for h in range(2):
            for first in (0, 2):
                groups.append([(1, a, j, h, True) for a in range(first, first + 2) for j in range(SLOTS)])

        idle = keep.tile([P, WARM_N], F32, name="idle")
        nc.vector.memset(idle[:], 0.0)
        idle_bf16 = idle[:].bitcast(BF16)

        for n in range(3):
            unread = psum.tile([P, N_TILE], F32, tag="acc")
            nc.tensor.matmul(unread[:, :WARM_N], idle[:, :P], idle[:], start=True, stop=True)
        for unit in order[:4]:
            turn(unit)
            unread = psum.tile([P, N_TILE], F32, tag="acc")
            nc.tensor.matmul(unread[:, :HOLD_N], idle_bf16[:, :P], idle_bf16[:, :HOLD_N], start=True, stop=True)
            for g in range(PASSES):
                quantise(unit, g)

        turn(order[4])
        deinterleave(order[6], nc.scalar.copy)
        for g in range(PASSES):
            quantise(order[4], g)
        for tile in groups[0][:2]:
            tile_and_store(*tile)
        deinterleave(order[7], nc.vector.tensor_copy)
        turn(order[5])
        for g in range(PASSES):
            quantise(order[5], g)
        for tile in groups[0][2:]:
            tile_and_store(*tile)

        turn_before = {1: order[6:8], 3: order[8:10], 4: order[10:11], 5: order[11:12]}
        split_during = {1: order[8:11], 3: order[11:12]}
        for n in range(1, len(groups)):
            pending = []
            for unit in turn_before.get(n, []):
                turn(unit)
                pending.extend([(unit, g) for g in range(PASSES)])
            for unit in split_during.get(n, []):
                deinterleave(unit, nc.scalar.copy)
            quantise_before_tile = (2, 1, 1, 0) if len(pending) == 4 else (0, 1, 1, 0)
            for i, tile in enumerate(groups[n]):
                first = sum(quantise_before_tile[:i])
                for unit, g in pending[first : first + quantise_before_tile[i]]:
                    quantise(unit, g)
                tile_and_store(*tile)
